import numpy as np
import ml_dtypes


def mxq(x, axis, fmt="e4m3"):
    dtype, down = {"e4m3": (ml_dtypes.float8_e4m3fn, 7), "e5m2": (ml_dtypes.float8_e5m2, 14)}[fmt]
    v = np.moveaxis(np.asarray(x, np.float32).astype(ml_dtypes.bfloat16).astype(np.float64), axis, -1)
    blocks = v.reshape(v.shape[:-1] + (-1, 32))
    amax = np.abs(blocks).max(-1, keepdims=True)
    byte = np.maximum(np.where(amax > 0, np.frexp(amax)[1] - 1 + 127, 0) - down, 1)
    scale = np.exp2(byte - 127.0)
    codes = (blocks / scale).astype(np.float32).astype(dtype).astype(np.float64)
    return np.moveaxis((codes * scale).reshape(v.shape), -1, axis)


WIDE = False


def mx_kscale(k):
    if not WIDE:
        return np.ones(k)
    levels = np.array([10, -10, 5, -5, 0])
    a = np.random.permutation(np.resize(levels, k // 512 * 4)).reshape(k // 512, 4)
    idx = np.arange(k)
    return np.exp2(a[idx // 512, idx % 128 // 32])


BF16 = ml_dtypes.bfloat16


def bf(x):
    return np.asarray(x, np.float32).astype(BF16)


def f64(x):
    return np.asarray(x).astype(np.float64)


E2M1 = np.array([0.0, 0.5, 1.0, 1.5, 2.0, 3.0, 4.0, 6.0, -0.0, -0.5, -1.0, -1.5, -2.0, -3.0, -4.0, -6.0])


def pack_weight(w, fmt):
    k, n = w.shape
    w = f64(bf(w)).reshape(k // 32, 32, n)
    amax = np.abs(w).max(1)
    if fmt == "e4m3":
        byte = np.frexp(amax)[1] - 1 + 127 - 7
    else:
        mant, ex = np.frexp(amax / 6.0)
        byte = np.where(mant > 0.5, ex, ex - 1) + 127
    byte = np.clip(np.where(amax > 0, byte, 1), 1, 254)
    scaled = (w * np.exp2(127.0 - byte)[:, None, :]).reshape(k, n).astype(np.float32)
    by_word = np.ascontiguousarray(scaled.reshape(k // 512, 128, 4, n).transpose(0, 1, 3, 2))
    if fmt == "e4m3":
        words = by_word.astype(ml_dtypes.float8_e4m3fn).view(np.uint8)
    else:
        c = by_word.astype(ml_dtypes.float4_e2m1fn).view(np.uint8) & 0xF
        words = c[..., 0::2] | (c[..., 1::2] << 4)
    return np.ascontiguousarray(words), np.ascontiguousarray(byte.astype(np.uint8).reshape(k // 512, 16, n))


def unpack_weight(words, scales, fmt):
    g, p, n, _ = words.shape
    if fmt == "e4m3":
        vals = np.ascontiguousarray(words).view(ml_dtypes.float8_e4m3fn).astype(np.float64)
    else:
        nib = np.empty((g, p, n, 4), np.uint8)
        nib[..., 0::2] = words & 0xF
        nib[..., 1::2] = words >> 4
        vals = E2M1[nib]
    vals = vals * np.repeat(np.exp2(scales.astype(np.float64) - 127.0), 8, axis=1)[..., None]
    return vals.transpose(0, 1, 3, 2).reshape(g * 512, n)


B, T, H, DK, DH, E, V = 128, 1, 24, 64, 64, 1536, 1536
HK = H * DK
FMT = "e4m3"


def rotate_every_two(u):
    u1 = u[..., ::2]
    u2 = u[..., 1::2]
    return np.stack((-u2, u1), axis=-1).reshape(u.shape)


def theta_shift(u, sin, cos):
    return u * cos + rotate_every_two(u) * sin


def setup_inputs():
    s = mx_kscale(E)
    x = bf(np.random.standard_normal((B, T, E)) * s)
    sin = bf(np.random.standard_normal((T, DK)) * 0.7)
    cos = bf(np.random.standard_normal((T, DK)) * 0.7)
    Wq_words, Wq_scales = pack_weight(np.random.standard_normal((E, HK)) / np.sqrt(E) / s[:, None], FMT)
    Wk_words, Wk_scales = pack_weight(np.random.standard_normal((E, HK)) / np.sqrt(E) / s[:, None], FMT)
    return {"x": x,
            "sin": sin,
            "cos": cos,
            "Wq_words": Wq_words,
            "Wq_scales": Wq_scales,
            "Wk_words": Wk_words,
            "Wk_scales": Wk_scales}


def reference(x, sin, cos, Wq_words, Wq_scales, Wk_words, Wk_scales):
    xq = mxq(f64(x), 2, "e4m3")
    q = (xq @ unpack_weight(Wq_words, Wq_scales, FMT)).reshape(B, T, H, DK).transpose(0, 2, 1, 3)
    k = (xq @ unpack_weight(Wk_words, Wk_scales, FMT)).reshape(B, T, H, DK).transpose(0, 2, 1, 3)
    qr = theta_shift(q, f64(sin), f64(cos))
    kr = theta_shift(k, f64(sin), f64(cos))
    return qr, kr

@@ -1,0 +1,146 @@
+from contextlib import ExitStack
+
+import concourse.mybir as mybir
+from concourse.masks import make_identity
+
+BF16 = mybir.dt.bfloat16
+F32 = mybir.dt.float32
+I32 = mybir.dt.int32
+U8 = mybir.dt.uint8
+U32 = mybir.dt.uint32
+FP8X4 = mybir.dt.float8_e4m3fn_x4
+
+P = 128
+PACK = 4
+K_PASS = P * PACK
+E = 1536
+PASSES = E // K_PASS
+WIDTH = 1536
+CHANNELS = 64
+PAIRS = CHANNELS // 2
+N_TILE = 512
+TILES = WIDTH // N_TILE
+HEADS = N_TILE // CHANNELS
+SCALE_ROWS = 4
+QUADRANTS = 4
+
+FLOPS = 2 * P * E * 2 * WIDTH
+
+
+def tile_multiscaleretention_pa_kernel(
+    tc, x, sin, cos, Wq_words, Wq_scales, Wk_words, Wk_scales, out_0, out_1
+):
+    nc = tc.nc
+    weights = ((Wq_words, Wq_scales), (Wk_words, Wk_scales))
+    outputs = (out_0, out_1)
+
+    with ExitStack() as ctx:
+        keep = ctx.enter_context(tc.tile_pool(name="keep", bufs=1))
+        words_pool = ctx.enter_context(tc.tile_pool(name="words", bufs=2 * TILES))
+        work = ctx.enter_context(tc.tile_pool(name="work", bufs=3))
+        psum_x = ctx.enter_context(tc.psum_pool(name="psum_x", bufs=PASSES))
+        psum_tables = ctx.enter_context(tc.psum_pool(name="psum_tables", bufs=1))
+        psum_acc = ctx.enter_context(tc.psum_pool(name="psum_acc", bufs=4))
+
+        planes = keep.tile([P, 2, WIDTH], U8, align_bytes=64)
+        nc.vector.memset(planes[:].bitcast(I32), 0)
+        table_row = keep.tile([P, 2 * CHANNELS], BF16)
+        nc.vector.memset(table_row[:], 0.0)
+        ones = keep.tile([P, P], BF16)
+        nc.vector.memset(ones[:], 1.0)
+        identity = keep.tile([P, P], F32)
+        make_identity(nc, identity[:])
+
+        x_sb = keep.tile([P, E], BF16)
+        nc.sync.dma_start(out=x_sb[:], in_=x.rearrange("b t e -> b (t e)"))
+        nc.scalar.dma_start(out=table_row[0:1, 0:CHANNELS], in_=sin)
+        nc.scalar.dma_start(out=table_row[0:1, CHANNELS : 2 * CHANNELS], in_=cos)
+
+        words = []
+        for w, (w_words, w_scales) in enumerate(weights):
+            for quadrant in range(QUADRANTS):
+                first = 32 * quadrant
+                nc.sync.dma_start(
+                    out=planes[first : first + PASSES * SCALE_ROWS, w, :].bitcast(I32),
+                    in_=w_scales[
+                        :, SCALE_ROWS * quadrant : SCALE_ROWS * (quadrant + 1), :
+                    ].bitcast(I32),
+                )
+            by_partition = w_words.rearrange("g p n t -> p g (n t)")
+            for j in range(TILES):
+                tile_words = words_pool.tile([P, PASSES, N_TILE], U32, align_bytes=64)
+                nc.sync.dma_start(
+                    out=tile_words[:].bitcast(I32),
+                    in_=by_partition[:, :, PACK * N_TILE * j : PACK * N_TILE * (j + 1)].bitcast(I32),
+                )
+                words.append(tile_words)
+
+        spread = psum_tables.tile([P, 2 * CHANNELS], F32)
+        nc.tensor.matmul(out=spread[:], lhsT=ones[:], rhs=table_row[:], start=True, stop=True)
+        cos_table = keep.tile([P, CHANNELS], F32)
+        nc.vector.tensor_copy(out=cos_table[:], in_=spread[:, CHANNELS : 2 * CHANNELS])
+        sin_by_parity = spread[:, 0:CHANNELS].rearrange("p (i e) -> p e i", e=2)
+        signed_sin = keep.tile([P, 2, PAIRS], F32)
+        nc.vector.tensor_scalar_mul(out=signed_sin[:, 0, :], in0=sin_by_parity[:, 0, :], scalar1=-1.0)
+        nc.vector.tensor_copy(out=signed_sin[:, 1, :], in_=sin_by_parity[:, 1, :])
+
+        x_pairs = x_sb[:].bitcast(F32)
+        grouped = keep.tile([P, PASSES, P, PACK], BF16, align_bytes=64)
+        x_codes = keep.tile([P, PASSES, P], U32, align_bytes=64)
+        x_scales = keep.tile([P, PASSES, P], U8, align_bytes=64)
+        pairs_per_pass = K_PASS // 2
+        for g in range(PASSES):
+            flipped = psum_x.tile([P, 2, P], F32)
+            for u in range(2):
+                nc.tensor.transpose(
+                    flipped[:, u, :],
+                    x_pairs[:, pairs_per_pass * g + u : pairs_per_pass * (g + 1) : 2],
+                    identity[:],
+                )
+            nc.scalar.copy(
+                out=grouped[:, g].bitcast(F32), in_=flipped[:].rearrange("p u b -> p b u")
+            )
+        for g in range(PASSES):
+            nc.vector.quantize_mx(
+                out=x_codes[:, g, :].bitcast(FP8X4),
+                scales=x_scales[:, g, :],
+                in_=grouped[:, g].rearrange("p b t -> p (b t)"),
+            )
+
+        for w, out in enumerate(outputs):
+            out_rows = out.rearrange("b h t c -> b (h t c)")
+            for j in range(TILES):
+                columns = slice(N_TILE * j, N_TILE * (j + 1))
+                acc = psum_acc.tile([P, N_TILE], F32)
+                for g in range(PASSES):
+                    nc.tensor.matmul_mx(
+                        out=acc[:],
+                        lhsT=x_codes[:, g, :].bitcast(FP8X4),
+                        lhsT_scale=x_scales[:, g, :],
+                        rhs=words[TILES * w + j][:, g, :].bitcast(FP8X4),
+                        rhs_scale=planes[SCALE_ROWS * g : P, w, columns],
+                        start=(g == 0),
+                        stop=(g == PASSES - 1),
+                    )
+
+                straight = work.tile([P, N_TILE], F32)
+                nc.vector.tensor_mul(
+                    out=straight[:].rearrange("p (h c) -> p h c", c=CHANNELS),
+                    in0=acc[:].rearrange("p (h c) -> p h c", c=CHANNELS),
+                    in1=cos_table[:].unsqueeze(1).to_broadcast([P, HEADS, CHANNELS]),
+                )
+                by_parity = acc[:].rearrange("p (h i e) -> p e h i", i=PAIRS, e=2)
+                crossed = work.tile([P, 2, N_TILE // 2], F32)
+                for e in range(2):
+                    nc.vector.tensor_mul(
+                        out=crossed[:, e, :].rearrange("p (h i) -> p h i", i=PAIRS),
+                        in0=by_parity[:, 1 - e],
+                        in1=signed_sin[:, e, :].unsqueeze(1).to_broadcast([P, HEADS, PAIRS]),
+                    )
+                rotated = work.tile([P, N_TILE], F32)
+                nc.gpsimd.tensor_add(
+                    out=rotated[:].rearrange("p (m e) -> p m e", e=2),
+                    in0=straight[:].rearrange("p (m e) -> p m e", e=2),
+                    in1=crossed[:].rearrange("p e m -> p m e"),
+                )
+                nc.scalar.dma_start(out=out_rows[:, columns], in_=rotated[:])

@@ -143,4 +143,4 @@ def tile_multiscaleretention_pa_kernel(
                     in0=straight[:].rearrange("p (m e) -> p m e", e=2),
                     in1=crossed[:].rearrange("p e m -> p m e"),
                 )
-                nc.scalar.dma_start(out=out_rows[:, columns], in_=rotated[:])
+                nc.sync.dma_start(out=out_rows[:, columns], in_=rotated[:])

@@ -18,9 +18,7 @@ PASSES = E // K_PASS
 WIDTH = 1536
 CHANNELS = 64
 PAIRS = CHANNELS // 2
-N_TILE = 512
-TILES = WIDTH // N_TILE
-HEADS = N_TILE // CHANNELS
+BANK = 512
 SCALE_ROWS = 4
 QUADRANTS = 4
 
@@ -34,55 +32,58 @@ def tile_multiscaleretention_pa_kernel(
     weights = ((Wq_words, Wq_scales), (Wk_words, Wk_scales))
     outputs = (out_0, out_1)
 
+    banks = [(w, first) for w in range(2) for first in range(0, WIDTH, BANK)]
+    pieces = [(w, first, BANK) for w, first in banks[:-1]]
+    last_w, last_first = banks[-1]
+    pieces.append((last_w, last_first, BANK // 2))
+    pieces.append((last_w, last_first + BANK // 2, BANK // 2))
+
     with ExitStack() as ctx:
         keep = ctx.enter_context(tc.tile_pool(name="keep", bufs=1))
-        words_pool = ctx.enter_context(tc.tile_pool(name="words", bufs=2 * TILES))
+        words_pool = ctx.enter_context(tc.tile_pool(name="words", bufs=len(pieces)))
         work = ctx.enter_context(tc.tile_pool(name="work", bufs=3))
+        results = ctx.enter_context(tc.tile_pool(name="results", bufs=len(pieces)))
         psum_x = ctx.enter_context(tc.psum_pool(name="psum_x", bufs=PASSES))
         psum_tables = ctx.enter_context(tc.psum_pool(name="psum_tables", bufs=1))
         psum_acc = ctx.enter_context(tc.psum_pool(name="psum_acc", bufs=4))
+        ctx.enter_context(tc.manual_schedule())
 
-        planes = keep.tile([P, 2, WIDTH], U8, align_bytes=64)
-        nc.vector.memset(planes[:].bitcast(I32), 0)
         table_row = keep.tile([P, 2 * CHANNELS], BF16)
         nc.vector.memset(table_row[:], 0.0)
+        planes = keep.tile([P, 2, WIDTH], U8, align_bytes=64)
+        nc.vector.memset(planes[:].bitcast(I32), 0)
         ones = keep.tile([P, P], BF16)
         nc.vector.memset(ones[:], 1.0)
+
         identity = keep.tile([P, P], F32)
         make_identity(nc, identity[:])
+        nc.gpsimd.dma_start(out=table_row[0:1, 0:CHANNELS], in_=sin)
+        nc.gpsimd.dma_start(out=table_row[0:1, CHANNELS : 2 * CHANNELS], in_=cos)
 
         x_sb = keep.tile([P, E], BF16)
         nc.sync.dma_start(out=x_sb[:], in_=x.rearrange("b t e -> b (t e)"))
-        nc.scalar.dma_start(out=table_row[0:1, 0:CHANNELS], in_=sin)
-        nc.scalar.dma_start(out=table_row[0:1, CHANNELS : 2 * CHANNELS], in_=cos)
 
         words = []
         for w, (w_words, w_scales) in enumerate(weights):
             for quadrant in range(QUADRANTS):
-                first = 32 * quadrant
-                nc.sync.dma_start(
-                    out=planes[first : first + PASSES * SCALE_ROWS, w, :].bitcast(I32),
+                top = 32 * quadrant
+                nc.scalar.dma_start(
+                    out=planes[top : top + PASSES * SCALE_ROWS, w, :].bitcast(F32),
                     in_=w_scales[
                         :, SCALE_ROWS * quadrant : SCALE_ROWS * (quadrant + 1), :
-                    ].bitcast(I32),
+                    ].bitcast(F32),
                 )
             by_partition = w_words.rearrange("g p n t -> p g (n t)")
-            for j in range(TILES):
-                tile_words = words_pool.tile([P, PASSES, N_TILE], U32, align_bytes=64)
-                nc.sync.dma_start(
-                    out=tile_words[:].bitcast(I32),
-                    in_=by_partition[:, :, PACK * N_TILE * j : PACK * N_TILE * (j + 1)].bitcast(I32),
-                )
-                words.append(tile_words)
-
-        spread = psum_tables.tile([P, 2 * CHANNELS], F32)
-        nc.tensor.matmul(out=spread[:], lhsT=ones[:], rhs=table_row[:], start=True, stop=True)
-        cos_table = keep.tile([P, CHANNELS], F32)
-        nc.vector.tensor_copy(out=cos_table[:], in_=spread[:, CHANNELS : 2 * CHANNELS])
-        sin_by_parity = spread[:, 0:CHANNELS].rearrange("p (i e) -> p e i", e=2)
-        signed_sin = keep.tile([P, 2, PAIRS], F32)
-        nc.vector.tensor_scalar_mul(out=signed_sin[:, 0, :], in0=sin_by_parity[:, 0, :], scalar1=-1.0)
-        nc.vector.tensor_copy(out=signed_sin[:, 1, :], in_=sin_by_parity[:, 1, :])
+            for piece_w, first, width in pieces:
+                if piece_w == w:
+                    piece_words = words_pool.tile(
+                        [P, PASSES, width], U32, tag="words", align_bytes=64
+                    )
+                    nc.sync.dma_start(
+                        out=piece_words[:].bitcast(I32),
+                        in_=by_partition[:, :, PACK * first : PACK * (first + width)].bitcast(I32),
+                    )
+                    words.append(piece_words)
 
         x_pairs = x_sb[:].bitcast(F32)
         grouped = keep.tile([P, PASSES, P, PACK], BF16, align_bytes=64)
@@ -97,7 +98,7 @@ def tile_multiscaleretention_pa_kernel(
                     x_pairs[:, pairs_per_pass * g + u : pairs_per_pass * (g + 1) : 2],
                     identity[:],
                 )
-            nc.scalar.copy(
+            nc.vector.tensor_copy(
                 out=grouped[:, g].bitcast(F32), in_=flipped[:].rearrange("p u b -> p b u")
             )
         for g in range(PASSES):
@@ -107,40 +108,59 @@ def tile_multiscaleretention_pa_kernel(
                 in_=grouped[:, g].rearrange("p b t -> p (b t)"),
             )
 
-        for w, out in enumerate(outputs):
-            out_rows = out.rearrange("b h t c -> b (h t c)")
-            for j in range(TILES):
-                columns = slice(N_TILE * j, N_TILE * (j + 1))
-                acc = psum_acc.tile([P, N_TILE], F32)
-                for g in range(PASSES):
-                    nc.tensor.matmul_mx(
-                        out=acc[:],
-                        lhsT=x_codes[:, g, :].bitcast(FP8X4),
-                        lhsT_scale=x_scales[:, g, :],
-                        rhs=words[TILES * w + j][:, g, :].bitcast(FP8X4),
-                        rhs_scale=planes[SCALE_ROWS * g : P, w, columns],
-                        start=(g == 0),
-                        stop=(g == PASSES - 1),
-                    )
+        def project(piece):
+            w, first, width = pieces[piece]
+            acc = psum_acc.tile([P, width], F32, tag="acc")
+            for g in range(PASSES):
+                nc.tensor.matmul_mx(
+                    out=acc[:],
+                    lhsT=x_codes[:, g, :].bitcast(FP8X4),
+                    lhsT_scale=x_scales[:, g, :],
+                    rhs=words[piece][:, g, :].bitcast(FP8X4),
+                    rhs_scale=planes[SCALE_ROWS * g : P, w, first : first + width],
+                    start=(g == 0),
+                    stop=(g == PASSES - 1),
+                )
+            return acc
 
-                straight = work.tile([P, N_TILE], F32)
+        def rotate(piece, acc):
+            w, first, width = pieces[piece]
+            heads = width // CHANNELS
+            straight = work.tile([P, width], F32, tag="straight")
+            nc.vector.tensor_mul(
+                out=straight[:].rearrange("p (h c) -> p h c", c=CHANNELS),
+                in0=acc[:].rearrange("p (h c) -> p h c", c=CHANNELS),
+                in1=cos_table[:].unsqueeze(1).to_broadcast([P, heads, CHANNELS]),
+            )
+            by_parity = acc[:].rearrange("p (h i e) -> p e h i", i=PAIRS, e=2)
+            crossed = work.tile([P, 2, width // 2], F32, tag="crossed")
+            for e in range(2):
                 nc.vector.tensor_mul(
-                    out=straight[:].rearrange("p (h c) -> p h c", c=CHANNELS),
-                    in0=acc[:].rearrange("p (h c) -> p h c", c=CHANNELS),
-                    in1=cos_table[:].unsqueeze(1).to_broadcast([P, HEADS, CHANNELS]),
+                    out=crossed[:, e, :].rearrange("p (h i) -> p h i", i=PAIRS),
+                    in0=by_parity[:, 1 - e],
+                    in1=signed_sin[:, e, :].unsqueeze(1).to_broadcast([P, heads, PAIRS]),
                 )
-                by_parity = acc[:].rearrange("p (h i e) -> p e h i", i=PAIRS, e=2)
-                crossed = work.tile([P, 2, N_TILE // 2], F32)
-                for e in range(2):
-                    nc.vector.tensor_mul(
-                        out=crossed[:, e, :].rearrange("p (h i) -> p h i", i=PAIRS),
-                        in0=by_parity[:, 1 - e],
-                        in1=signed_sin[:, e, :].unsqueeze(1).to_broadcast([P, HEADS, PAIRS]),
-                    )
-                rotated = work.tile([P, N_TILE], F32)
-                nc.gpsimd.tensor_add(
-                    out=rotated[:].rearrange("p (m e) -> p m e", e=2),
-                    in0=straight[:].rearrange("p (m e) -> p m e", e=2),
-                    in1=crossed[:].rearrange("p e m -> p m e"),
-                )
-                nc.sync.dma_start(out=out_rows[:, columns], in_=rotated[:])
+            adder = nc.vector if piece == len(pieces) - 1 else nc.gpsimd
+            rotated = results.tile([P, width], F32, tag="rotated")
+            adder.tensor_add(
+                out=rotated[:].rearrange("p (m e) -> p m e", e=2),
+                in0=straight[:].rearrange("p (m e) -> p m e", e=2),
+                in1=crossed[:].rearrange("p e m -> p m e"),
+            )
+            out_rows = outputs[w].rearrange("b h t c -> b (h t c)")
+            nc.sync.dma_start(out=out_rows[:, first : first + width], in_=rotated[:])
+
+        first_acc = project(0)
+
+        spread = psum_tables.tile([P, 2 * CHANNELS], F32)
+        nc.tensor.matmul(out=spread[:], lhsT=ones[:], rhs=table_row[:], start=True, stop=True)
+        cos_table = keep.tile([P, CHANNELS], F32)
+        nc.vector.tensor_copy(out=cos_table[:], in_=spread[:, CHANNELS : 2 * CHANNELS])
+        sin_by_parity = spread[:, 0:CHANNELS].rearrange("p (i e) -> p e i", e=2)
+        signed_sin = keep.tile([P, 2, PAIRS], F32)
+        nc.vector.tensor_scalar_mul(out=signed_sin[:, 0, :], in0=sin_by_parity[:, 0, :], scalar1=-1.0)
+        nc.vector.tensor_copy(out=signed_sin[:, 1, :], in_=sin_by_parity[:, 1, :])
+
+        rotate(0, first_acc)
+        for piece in range(1, len(pieces)):
+            rotate(piece, project(piece))

@@ -140,9 +140,8 @@ def tile_multiscaleretention_pa_kernel(
                     in0=by_parity[:, 1 - e],
                     in1=signed_sin[:, e, :].unsqueeze(1).to_broadcast([P, heads, PAIRS]),
                 )
-            adder = nc.vector if piece == len(pieces) - 1 else nc.gpsimd
             rotated = results.tile([P, width], F32, tag="rotated")
-            adder.tensor_add(
+            nc.vector.tensor_add(
                 out=rotated[:].rearrange("p (m e) -> p m e", e=2),
                 in0=straight[:].rearrange("p (m e) -> p m e", e=2),
                 in1=crossed[:].rearrange("p e m -> p m e"),

@@ -57,39 +57,46 @@ def tile_multiscaleretention_pa_kernel(
 
         identity = keep.tile([P, P], F32)
         make_identity(nc, identity[:])
-        nc.gpsimd.dma_start(out=table_row[0:1, 0:CHANNELS], in_=sin)
-        nc.gpsimd.dma_start(out=table_row[0:1, CHANNELS : 2 * CHANNELS], in_=cos)
+        nc.scalar.dma_start(out=table_row[0:1, 0:CHANNELS], in_=sin)
+        nc.scalar.dma_start(out=table_row[0:1, CHANNELS : 2 * CHANNELS], in_=cos)
 
         x_sb = keep.tile([P, E], BF16)
         nc.sync.dma_start(out=x_sb[:], in_=x.rearrange("b t e -> b (t e)"))
 
         words = []
-        for w, (w_words, w_scales) in enumerate(weights):
-            for quadrant in range(QUADRANTS):
-                top = 32 * quadrant
-                nc.scalar.dma_start(
-                    out=planes[top : top + PASSES * SCALE_ROWS, w, :].bitcast(F32),
-                    in_=w_scales[
-                        :, SCALE_ROWS * quadrant : SCALE_ROWS * (quadrant + 1), :
-                    ].bitcast(F32),
-                )
-            by_partition = w_words.rearrange("g p n t -> p g (n t)")
-            for piece_w, first, width in pieces:
-                if piece_w == w:
-                    piece_words = words_pool.tile(
-                        [P, PASSES, width], U32, tag="words", align_bytes=64
-                    )
+        for w, first, width in pieces:
+            w_words, w_scales = weights[w]
+            piece_words = words_pool.tile([P, PASSES, width], U32, tag="words", align_bytes=64)
+            nc.sync.dma_start(
+                out=piece_words[:].bitcast(I32),
+                in_=w_words.rearrange("g p n t -> p g (n t)")[
+                    :, :, PACK * first : PACK * (first + width)
+                ].bitcast(I32),
+            )
+            words.append(piece_words)
+            if first == 0:
+                for quadrant in range(QUADRANTS):
+                    top = 32 * quadrant
                     nc.sync.dma_start(
-                        out=piece_words[:].bitcast(I32),
-                        in_=by_partition[:, :, PACK * first : PACK * (first + width)].bitcast(I32),
+                        out=planes[top : top + PASSES * SCALE_ROWS, w, :].bitcast(I32),
+                        in_=w_scales[
+                            :, SCALE_ROWS * quadrant : SCALE_ROWS * (quadrant + 1), :
+                        ].bitcast(I32),
                     )
-                    words.append(piece_words)
 
         x_pairs = x_sb[:].bitcast(F32)
         grouped = keep.tile([P, PASSES, P, PACK], BF16, align_bytes=64)
         x_codes = keep.tile([P, PASSES, P], U32, align_bytes=64)
         x_scales = keep.tile([P, PASSES, P], U8, align_bytes=64)
         pairs_per_pass = K_PASS // 2
+
+        def quantise(g):
+            nc.vector.quantize_mx(
+                out=x_codes[:, g, :].bitcast(FP8X4),
+                scales=x_scales[:, g, :],
+                in_=grouped[:, g].rearrange("p b t -> p (b t)"),
+            )
+
         for g in range(PASSES):
             flipped = psum_x.tile([P, 2, P], F32)
             for u in range(2):
@@ -101,12 +108,9 @@ def tile_multiscaleretention_pa_kernel(
             nc.vector.tensor_copy(
                 out=grouped[:, g].bitcast(F32), in_=flipped[:].rearrange("p u b -> p b u")
             )
-        for g in range(PASSES):
-            nc.vector.quantize_mx(
-                out=x_codes[:, g, :].bitcast(FP8X4),
-                scales=x_scales[:, g, :],
-                in_=grouped[:, g].rearrange("p b t -> p (b t)"),
-            )
+            if g > 0:
+                quantise(g - 1)
+        quantise(PASSES - 1)
 
         def project(piece):
             w, first, width = pieces[piece]
@@ -140,16 +144,15 @@ def tile_multiscaleretention_pa_kernel(
                     in0=by_parity[:, 1 - e],
                     in1=signed_sin[:, e, :].unsqueeze(1).to_broadcast([P, heads, PAIRS]),
                 )
+            adder = nc.vector if piece == len(pieces) - 1 else nc.gpsimd
             rotated = results.tile([P, width], F32, tag="rotated")
-            nc.vector.tensor_add(
+            adder.tensor_add(
                 out=rotated[:].rearrange("p (m e) -> p m e", e=2),
                 in0=straight[:].rearrange("p (m e) -> p m e", e=2),
                 in1=crossed[:].rearrange("p e m -> p m e"),
             )
             out_rows = outputs[w].rearrange("b h t c -> b (h t c)")
             nc.sync.dma_start(out=out_rows[:, first : first + width], in_=rotated[:])
-
-        first_acc = project(0)
 
         spread = psum_tables.tile([P, 2 * CHANNELS], F32)
         nc.tensor.matmul(out=spread[:], lhsT=ones[:], rhs=table_row[:], start=True, stop=True)
@@ -160,6 +163,5 @@ def tile_multiscaleretention_pa_kernel(
         nc.vector.tensor_scalar_mul(out=signed_sin[:, 0, :], in0=sin_by_parity[:, 0, :], scalar1=-1.0)
         nc.vector.tensor_copy(out=signed_sin[:, 1, :], in_=sin_by_parity[:, 1, :])
 
-        rotate(0, first_acc)
-        for piece in range(1, len(pieces)):
+        for piece in range(len(pieces)):
             rotate(piece, project(piece))

@@ -19,6 +19,8 @@ WIDTH = 1536
 CHANNELS = 64
 PAIRS = CHANNELS // 2
 BANK = 512
+NARROW = 128
+VECTOR_SUMS = 2
 SCALE_ROWS = 4
 QUADRANTS = 4
 
@@ -33,16 +35,24 @@ def tile_multiscaleretention_pa_kernel(
     outputs = (out_0, out_1)
 
     banks = [(w, first) for w in range(2) for first in range(0, WIDTH, BANK)]
-    pieces = [(w, first, BANK) for w, first in banks[:-1]]
-    last_w, last_first = banks[-1]
-    pieces.append((last_w, last_first, BANK // 2))
-    pieces.append((last_w, last_first + BANK // 2, BANK // 2))
+
+    rising = [NARROW]
+    while sum(rising) < BANK:
+        rising.append(sum(rising))
+    pieces = []
+    for bank in range(len(banks)):
+        widths = [BANK]
+        if bank == 0:
+            widths = rising
+        if bank == len(banks) - 1:
+            widths = list(reversed(rising))
+        for i, width in enumerate(widths):
+            pieces.append((bank, sum(widths[:i]), width))
 
     with ExitStack() as ctx:
         keep = ctx.enter_context(tc.tile_pool(name="keep", bufs=1))
-        words_pool = ctx.enter_context(tc.tile_pool(name="words", bufs=len(pieces)))
-        work = ctx.enter_context(tc.tile_pool(name="work", bufs=3))
-        results = ctx.enter_context(tc.tile_pool(name="results", bufs=len(pieces)))
+        words_pool = ctx.enter_context(tc.tile_pool(name="words", bufs=len(banks)))
+        work = ctx.enter_context(tc.tile_pool(name="work", bufs=len(pieces)))
         psum_x = ctx.enter_context(tc.psum_pool(name="psum_x", bufs=PASSES))
         psum_tables = ctx.enter_context(tc.psum_pool(name="psum_tables", bufs=1))
         psum_acc = ctx.enter_context(tc.psum_pool(name="psum_acc", bufs=4))
@@ -64,16 +74,16 @@ def tile_multiscaleretention_pa_kernel(
         nc.sync.dma_start(out=x_sb[:], in_=x.rearrange("b t e -> b (t e)"))
 
         words = []
-        for w, first, width in pieces:
+        for w, first in banks:
             w_words, w_scales = weights[w]
-            piece_words = words_pool.tile([P, PASSES, width], U32, tag="words", align_bytes=64)
+            bank_words = words_pool.tile([P, PASSES, BANK], U32, align_bytes=64)
             nc.sync.dma_start(
-                out=piece_words[:].bitcast(I32),
+                out=bank_words[:].bitcast(I32),
                 in_=w_words.rearrange("g p n t -> p g (n t)")[
-                    :, :, PACK * first : PACK * (first + width)
+                    :, :, PACK * first : PACK * (first + BANK)
                 ].bitcast(I32),
             )
-            words.append(piece_words)
+            words.append(bank_words)
             if first == 0:
                 for quadrant in range(QUADRANTS):
                     top = 32 * quadrant
@@ -113,22 +123,24 @@ def tile_multiscaleretention_pa_kernel(
         quantise(PASSES - 1)
 
         def project(piece):
-            w, first, width = pieces[piece]
+            bank, start, width = pieces[piece]
+            w, first = banks[bank]
             acc = psum_acc.tile([P, width], F32, tag="acc")
             for g in range(PASSES):
                 nc.tensor.matmul_mx(
                     out=acc[:],
                     lhsT=x_codes[:, g, :].bitcast(FP8X4),
                     lhsT_scale=x_scales[:, g, :],
-                    rhs=words[piece][:, g, :].bitcast(FP8X4),
-                    rhs_scale=planes[SCALE_ROWS * g : P, w, first : first + width],
+                    rhs=words[bank][:, g, start : start + width].bitcast(FP8X4),
+                    rhs_scale=planes[SCALE_ROWS * g : P, w, first + start : first + start + width],
                     start=(g == 0),
                     stop=(g == PASSES - 1),
                 )
             return acc
 
         def rotate(piece, acc):
-            w, first, width = pieces[piece]
+            bank, start, width = pieces[piece]
+            w, first = banks[bank]
             heads = width // CHANNELS
             straight = work.tile([P, width], F32, tag="straight")
             nc.vector.tensor_mul(
@@ -144,15 +156,17 @@ def tile_multiscaleretention_pa_kernel(
                     in0=by_parity[:, 1 - e],
                     in1=signed_sin[:, e, :].unsqueeze(1).to_broadcast([P, heads, PAIRS]),
                 )
-            adder = nc.vector if piece == len(pieces) - 1 else nc.gpsimd
-            rotated = results.tile([P, width], F32, tag="rotated")
+            adder = nc.vector if piece >= len(pieces) - VECTOR_SUMS else nc.gpsimd
+            rotated = work.tile([P, width], F32, tag="rotated")
             adder.tensor_add(
                 out=rotated[:].rearrange("p (m e) -> p m e", e=2),
                 in0=straight[:].rearrange("p (m e) -> p m e", e=2),
                 in1=crossed[:].rearrange("p e m -> p m e"),
             )
             out_rows = outputs[w].rearrange("b h t c -> b (h t c)")
-            nc.sync.dma_start(out=out_rows[:, first : first + width], in_=rotated[:])
+            nc.sync.dma_start(
+                out=out_rows[:, first + start : first + start + width], in_=rotated[:]
+            )
 
         spread = psum_tables.tile([P, 2 * CHANNELS], F32)
         nc.tensor.matmul(out=spread[:], lhsT=ones[:], rhs=table_row[:], start=True, stop=True)

@@ -122,6 +122,8 @@ def tile_multiscaleretention_pa_kernel(
                 quantise(g - 1)
         quantise(PASSES - 1)
 
+        results = [keep.tile([P, WIDTH], F32, name="result_%d" % w) for w in range(2)]
+
         def project(piece):
             bank, start, width = pieces[piece]
             w, first = banks[bank]
@@ -157,16 +159,17 @@ def tile_multiscaleretention_pa_kernel(
                     in1=signed_sin[:, e, :].unsqueeze(1).to_broadcast([P, heads, PAIRS]),
                 )
             adder = nc.vector if piece >= len(pieces) - VECTOR_SUMS else nc.gpsimd
-            rotated = work.tile([P, width], F32, tag="rotated")
+            columns = slice(first + start, first + start + width)
             adder.tensor_add(
-                out=rotated[:].rearrange("p (m e) -> p m e", e=2),
+                out=results[w][:, columns].rearrange("p (m e) -> p m e", e=2),
                 in0=straight[:].rearrange("p (m e) -> p m e", e=2),
                 in1=crossed[:].rearrange("p e m -> p m e"),
             )
             out_rows = outputs[w].rearrange("b h t c -> b (h t c)")
-            nc.sync.dma_start(
-                out=out_rows[:, first + start : first + start + width], in_=rotated[:]
-            )
+            if w == 1:
+                nc.sync.dma_start(out=out_rows[:, columns], in_=results[w][:, columns])
+            elif first + start + width == WIDTH:
+                nc.sync.dma_start(out=out_rows, in_=results[w][:])
 
         spread = psum_tables.tile([P, 2 * CHANNELS], F32)
         nc.tensor.matmul(out=spread[:], lhsT=ones[:], rhs=table_row[:], start=True, stop=True)

@@ -20,7 +20,7 @@ CHANNELS = 64
 PAIRS = CHANNELS // 2
 BANK = 512
 NARROW = 128
-VECTOR_SUMS = 2
+VECTOR_SUMS = 3
 SCALE_ROWS = 4
 QUADRANTS = 4
 
@@ -140,9 +140,8 @@ def tile_multiscaleretention_pa_kernel(
                 )
             return acc
 
-        def rotate(piece, acc):
-            bank, start, width = pieces[piece]
-            w, first = banks[bank]
+        def multiply(piece, acc):
+            width = pieces[piece][2]
             heads = width // CHANNELS
             straight = work.tile([P, width], F32, tag="straight")
             nc.vector.tensor_mul(
@@ -158,7 +157,11 @@ def tile_multiscaleretention_pa_kernel(
                     in0=by_parity[:, 1 - e],
                     in1=signed_sin[:, e, :].unsqueeze(1).to_broadcast([P, heads, PAIRS]),
                 )
-            adder = nc.vector if piece >= len(pieces) - VECTOR_SUMS else nc.gpsimd
+            return straight, crossed
+
+        def add_and_store(piece, adder, straight, crossed):
+            bank, start, width = pieces[piece]
+            w, first = banks[bank]
             columns = slice(first + start, first + start + width)
             adder.tensor_add(
                 out=results[w][:, columns].rearrange("p (m e) -> p m e", e=2),
@@ -180,5 +183,12 @@ def tile_multiscaleretention_pa_kernel(
         nc.vector.tensor_scalar_mul(out=signed_sin[:, 0, :], in0=sin_by_parity[:, 0, :], scalar1=-1.0)
         nc.vector.tensor_copy(out=signed_sin[:, 1, :], in_=sin_by_parity[:, 1, :])
 
+        vector_from = len(pieces) - VECTOR_SUMS
+        products = []
         for piece in range(len(pieces)):
-            rotate(piece, project(piece))
+            products.append(multiply(piece, project(piece)))
+            if piece < vector_from:
+                add_and_store(piece, nc.gpsimd, *products[piece])
+            if piece > vector_from:
+                add_and_store(piece - 1, nc.vector, *products[piece - 1])
+        add_and_store(len(pieces) - 1, nc.vector, *products[-1])

@@ -19,10 +19,10 @@ WIDTH = 1536
 CHANNELS = 64
 PAIRS = CHANNELS // 2
 BANK = 512
-NARROW = 128
-VECTOR_SUMS = 3
 SCALE_ROWS = 4
 QUADRANTS = 4
+TURNED = 256
+DIRECT = BANK - TURNED
 
 FLOPS = 2 * P * E * 2 * WIDTH
 
@@ -36,26 +36,14 @@ def tile_multiscaleretention_pa_kernel(
 
     banks = [(w, first) for w in range(2) for first in range(0, WIDTH, BANK)]
 
-    rising = [NARROW]
-    while sum(rising) < BANK:
-        rising.append(sum(rising))
-    pieces = []
-    for bank in range(len(banks)):
-        widths = [BANK]
-        if bank == 0:
-            widths = rising
-        if bank == len(banks) - 1:
-            widths = list(reversed(rising))
-        for i, width in enumerate(widths):
-            pieces.append((bank, sum(widths[:i]), width))
-
     with ExitStack() as ctx:
         keep = ctx.enter_context(tc.tile_pool(name="keep", bufs=1))
         words_pool = ctx.enter_context(tc.tile_pool(name="words", bufs=len(banks)))
-        work = ctx.enter_context(tc.tile_pool(name="work", bufs=len(pieces)))
-        psum_x = ctx.enter_context(tc.psum_pool(name="psum_x", bufs=PASSES))
+        work = ctx.enter_context(tc.tile_pool(name="work", bufs=4))
+        psum_direct = ctx.enter_context(tc.psum_pool(name="psum_direct", bufs=3))
+        psum_turned = ctx.enter_context(tc.psum_pool(name="psum_turned", bufs=2))
+        psum_rotated = ctx.enter_context(tc.psum_pool(name="psum_rotated", bufs=2))
         psum_tables = ctx.enter_context(tc.psum_pool(name="psum_tables", bufs=1))
-        psum_acc = ctx.enter_context(tc.psum_pool(name="psum_acc", bufs=4))
         ctx.enter_context(tc.manual_schedule())
 
         table_row = keep.tile([P, 2 * CHANNELS], BF16)
@@ -67,6 +55,12 @@ def tile_multiscaleretention_pa_kernel(
 
         identity = keep.tile([P, P], F32)
         make_identity(nc, identity[:])
+        swap = keep.tile([P, P], F32)
+        identity_pairs = identity[:].rearrange("p (m e) -> p m e", e=2)
+        swap_pairs = swap[:].rearrange("p (m e) -> p m e", e=2)
+        nc.gpsimd.tensor_scalar_mul(out=swap_pairs[:, :, 0], in0=identity_pairs[:, :, 1], scalar1=-1.0)
+        nc.gpsimd.tensor_copy(out=swap_pairs[:, :, 1], in_=identity_pairs[:, :, 0])
+
         nc.scalar.dma_start(out=table_row[0:1, 0:CHANNELS], in_=sin)
         nc.scalar.dma_start(out=table_row[0:1, CHANNELS : 2 * CHANNELS], in_=cos)
 
@@ -100,34 +94,78 @@ def tile_multiscaleretention_pa_kernel(
         x_scales = keep.tile([P, PASSES, P], U8, align_bytes=64)
         pairs_per_pass = K_PASS // 2
 
-        def quantise(g):
-            nc.vector.quantize_mx(
-                out=x_codes[:, g, :].bitcast(FP8X4),
-                scales=x_scales[:, g, :],
-                in_=grouped[:, g].rearrange("p b t -> p (b t)"),
-            )
-
         for g in range(PASSES):
-            flipped = psum_x.tile([P, 2, P], F32)
+            flipped = psum_direct.tile([P, 2, P], F32, tag="direct")
             for u in range(2):
                 nc.tensor.transpose(
                     flipped[:, u, :],
                     x_pairs[:, pairs_per_pass * g + u : pairs_per_pass * (g + 1) : 2],
                     identity[:],
                 )
-            nc.vector.tensor_copy(
+            nc.scalar.copy(
                 out=grouped[:, g].bitcast(F32), in_=flipped[:].rearrange("p u b -> p b u")
             )
-            if g > 0:
-                quantise(g - 1)
-        quantise(PASSES - 1)
+            nc.vector.quantize_mx(
+                out=x_codes[:, g, :].bitcast(FP8X4),
+                scales=x_scales[:, g, :],
+                in_=grouped[:, g].rearrange("p b t -> p (b t)"),
+            )
 
         results = [keep.tile([P, WIDTH], F32, name="result_%d" % w) for w in range(2)]
 
-        def project(piece):
-            bank, start, width = pieces[piece]
+        spread = psum_tables.tile([P, 2 * CHANNELS], F32)
+        nc.tensor.matmul(out=spread[:], lhsT=ones[:], rhs=table_row[:], start=True, stop=True)
+        cos_table = keep.tile([P, CHANNELS], F32)
+        nc.vector.tensor_copy(out=cos_table[:], in_=spread[:, CHANNELS : 2 * CHANNELS])
+        sin_by_parity = spread[:, 0:CHANNELS].rearrange("p (i e) -> p e i", e=2)
+        signed_sin = keep.tile([P, 2, PAIRS], F32)
+        nc.vector.tensor_scalar_mul(out=signed_sin[:, 0, :], in0=sin_by_parity[:, 0, :], scalar1=-1.0)
+        nc.vector.tensor_copy(out=signed_sin[:, 1, :], in_=sin_by_parity[:, 1, :])
+        two_heads = [P, P // CHANNELS, CHANNELS]
+        on_diagonal = keep.tile([P, P], F32)
+        nc.vector.tensor_mul(
+            out=on_diagonal[:].rearrange("p (h c) -> p h c", c=CHANNELS),
+            in0=identity[:].rearrange("p (h c) -> p h c", c=CHANNELS),
+            in1=spread[:, CHANNELS : 2 * CHANNELS].unsqueeze(1).to_broadcast(two_heads),
+        )
+        beside = keep.tile([P, P], F32)
+        nc.vector.tensor_mul(
+            out=beside[:].rearrange("p (h c) -> p h c", c=CHANNELS),
+            in0=swap[:].rearrange("p (h c) -> p h c", c=CHANNELS),
+            in1=spread[:, 0:CHANNELS].unsqueeze(1).to_broadcast(two_heads),
+        )
+        rotation = keep.tile([P, P], F32)
+        nc.vector.tensor_add(out=rotation[:], in0=on_diagonal[:], in1=beside[:])
+
+        def turned_passes(bank, j):
             w, first = banks[bank]
-            acc = psum_acc.tile([P, width], F32, tag="acc")
+            column = DIRECT + P * j
+            turned = psum_turned.tile([P, P], F32, tag="turned")
+            for g in range(PASSES):
+                nc.tensor.matmul_mx(
+                    out=turned[:],
+                    lhsT=words[bank][:, g, column : column + P].bitcast(FP8X4),
+                    lhsT_scale=planes[SCALE_ROWS * g : P, w, first + column : first + column + P],
+                    rhs=x_codes[:, g, :].bitcast(FP8X4),
+                    rhs_scale=x_scales[:, g, :],
+                    start=(g == 0),
+                    stop=(g == PASSES - 1),
+                )
+            turned_sb = work.tile([P, P], F32, tag="turned_sb")
+            nc.scalar.copy(out=turned_sb[:], in_=turned[:])
+            return turned_sb
+
+        def rotate(bank, j, turned_sb):
+            w, first = banks[bank]
+            column = first + DIRECT + P * j
+            rotated = psum_rotated.tile([P, P], F32, tag="rotated")
+            nc.tensor.matmul(out=rotated[:], lhsT=turned_sb[:], rhs=rotation[:], start=True, stop=True)
+            nc.scalar.copy(out=results[w][:, column : column + P], in_=rotated[:])
+
+        def direct_passes(piece):
+            bank, start, width = piece
+            w, first = banks[bank]
+            acc = psum_direct.tile([P, width], F32, tag="direct")
             for g in range(PASSES):
                 nc.tensor.matmul_mx(
                     out=acc[:],
@@ -141,7 +179,7 @@ def tile_multiscaleretention_pa_kernel(
             return acc
 
         def multiply(piece, acc):
-            width = pieces[piece][2]
+            width = piece[2]
             heads = width // CHANNELS
             straight = work.tile([P, width], F32, tag="straight")
             nc.vector.tensor_mul(
@@ -159,36 +197,48 @@ def tile_multiscaleretention_pa_kernel(
                 )
             return straight, crossed
 
-        def add_and_store(piece, adder, straight, crossed):
-            bank, start, width = pieces[piece]
+        def add(piece, straight, crossed):
+            bank, start, width = piece
             w, first = banks[bank]
-            columns = slice(first + start, first + start + width)
-            adder.tensor_add(
-                out=results[w][:, columns].rearrange("p (m e) -> p m e", e=2),
+            nc.vector.tensor_add(
+                out=results[w][:, first + start : first + start + width].rearrange(
+                    "p (m e) -> p m e", e=2
+                ),
                 in0=straight[:].rearrange("p (m e) -> p m e", e=2),
                 in1=crossed[:].rearrange("p e m -> p m e"),
             )
+
+        def store(w, begin, end):
             out_rows = outputs[w].rearrange("b h t c -> b (h t c)")
-            if w == 1:
-                nc.sync.dma_start(out=out_rows[:, columns], in_=results[w][:, columns])
-            elif first + start + width == WIDTH:
-                nc.sync.dma_start(out=out_rows, in_=results[w][:])
+            nc.sync.dma_start(out=out_rows[:, begin:end], in_=results[w][:, begin:end])
 
-        spread = psum_tables.tile([P, 2 * CHANNELS], F32)
-        nc.tensor.matmul(out=spread[:], lhsT=ones[:], rhs=table_row[:], start=True, stop=True)
-        cos_table = keep.tile([P, CHANNELS], F32)
-        nc.vector.tensor_copy(out=cos_table[:], in_=spread[:, CHANNELS : 2 * CHANNELS])
-        sin_by_parity = spread[:, 0:CHANNELS].rearrange("p (i e) -> p e i", e=2)
-        signed_sin = keep.tile([P, 2, PAIRS], F32)
-        nc.vector.tensor_scalar_mul(out=signed_sin[:, 0, :], in0=sin_by_parity[:, 0, :], scalar1=-1.0)
-        nc.vector.tensor_copy(out=signed_sin[:, 1, :], in_=sin_by_parity[:, 1, :])
-
-        vector_from = len(pieces) - VECTOR_SUMS
+        last = len(banks) - 1
+        pieces = []
         products = []
-        for piece in range(len(pieces)):
-            products.append(multiply(piece, project(piece)))
-            if piece < vector_from:
-                add_and_store(piece, nc.gpsimd, *products[piece])
-            if piece > vector_from:
-                add_and_store(piece - 1, nc.vector, *products[piece - 1])
-        add_and_store(len(pieces) - 1, nc.vector, *products[-1])
+
+        def add_previous():
+            piece = pieces[len(products) - 2]
+            add(piece, *products[len(products) - 2])
+            bank, start, width = piece
+            w, first = banks[bank]
+            if start + width == DIRECT and bank < last:
+                if w == 1:
+                    store(w, first, first + BANK)
+                elif first + BANK == WIDTH:
+                    store(w, 0, WIDTH)
+
+        for bank in range(len(banks)):
+            blocks = [turned_passes(bank, j) for j in range(TURNED // P)]
+            widths = [DIRECT] if bank < last else [P] * (DIRECT // P)
+            for i, width in enumerate(widths):
+                piece = (bank, sum(widths[:i]), width)
+                pieces.append(piece)
+                products.append(multiply(piece, direct_passes(piece)))
+                if len(products) > 1:
+                    add_previous()
+            for j in range(TURNED // P):
+                rotate(bank, j, blocks[j])
+        w, first = banks[last]
+        store(w, first + DIRECT, first + BANK)
+        add(pieces[-1], *products[-1])
+        store(w, first, first + DIRECT)

@@ -21,8 +21,8 @@ PAIRS = CHANNELS // 2
 BANK = 512
 SCALE_ROWS = 4
 QUADRANTS = 4
-TURNED = 256
-DIRECT = BANK - TURNED
+TURNED = 128
+TURNED_LAST = 256
 
 FLOPS = 2 * P * E * 2 * WIDTH
 
@@ -115,12 +115,12 @@ def tile_multiscaleretention_pa_kernel(
 
         spread = psum_tables.tile([P, 2 * CHANNELS], F32)
         nc.tensor.matmul(out=spread[:], lhsT=ones[:], rhs=table_row[:], start=True, stop=True)
-        cos_table = keep.tile([P, CHANNELS], F32)
-        nc.vector.tensor_copy(out=cos_table[:], in_=spread[:, CHANNELS : 2 * CHANNELS])
-        sin_by_parity = spread[:, 0:CHANNELS].rearrange("p (i e) -> p e i", e=2)
-        signed_sin = keep.tile([P, 2, PAIRS], F32)
-        nc.vector.tensor_scalar_mul(out=signed_sin[:, 0, :], in0=sin_by_parity[:, 0, :], scalar1=-1.0)
-        nc.vector.tensor_copy(out=signed_sin[:, 1, :], in_=sin_by_parity[:, 1, :])
+        factors = keep.tile([P, 2, CHANNELS], F32)
+        nc.vector.tensor_copy(out=factors[:, 0, :], in_=spread[:, CHANNELS : 2 * CHANNELS])
+        sin_pairs = spread[:, 0:CHANNELS].rearrange("p (i e) -> p i e", e=2)
+        cross_pairs = factors[:, 1, :].rearrange("p (i e) -> p i e", e=2)
+        nc.vector.tensor_copy(out=cross_pairs[:, :, 0], in_=sin_pairs[:, :, 1])
+        nc.vector.tensor_scalar_mul(out=cross_pairs[:, :, 1], in0=sin_pairs[:, :, 0], scalar1=-1.0)
         two_heads = [P, P // CHANNELS, CHANNELS]
         on_diagonal = keep.tile([P, P], F32)
         nc.vector.tensor_mul(
@@ -137,9 +137,14 @@ def tile_multiscaleretention_pa_kernel(
         rotation = keep.tile([P, P], F32)
         nc.vector.tensor_add(out=rotation[:], in0=on_diagonal[:], in1=beside[:])
 
+        last = len(banks) - 1
+
+        def direct_of(bank):
+            return BANK - (TURNED_LAST if bank == last else TURNED)
+
         def turned_passes(bank, j):
             w, first = banks[bank]
-            column = DIRECT + P * j
+            column = direct_of(bank) + P * j
             turned = psum_turned.tile([P, P], F32, tag="turned")
             for g in range(PASSES):
                 nc.tensor.matmul_mx(
@@ -157,7 +162,7 @@ def tile_multiscaleretention_pa_kernel(
 
         def rotate(bank, j, turned_sb):
             w, first = banks[bank]
-            column = first + DIRECT + P * j
+            column = first + direct_of(bank) + P * j
             rotated = psum_rotated.tile([P, P], F32, tag="rotated")
             nc.tensor.matmul(out=rotated[:], lhsT=turned_sb[:], rhs=rotation[:], start=True, stop=True)
             nc.scalar.copy(out=results[w][:, column : column + P], in_=rotated[:])
@@ -180,39 +185,30 @@ def tile_multiscaleretention_pa_kernel(
 
         def multiply(piece, acc):
             width = piece[2]
-            heads = width // CHANNELS
-            straight = work.tile([P, width], F32, tag="straight")
+            shape = [P, 2, width // CHANNELS, CHANNELS]
+            both = work.tile([P, 2, width], F32, tag="both")
             nc.vector.tensor_mul(
-                out=straight[:].rearrange("p (h c) -> p h c", c=CHANNELS),
-                in0=acc[:].rearrange("p (h c) -> p h c", c=CHANNELS),
-                in1=cos_table[:].unsqueeze(1).to_broadcast([P, heads, CHANNELS]),
+                out=both[:].rearrange("p r (h c) -> p r h c", c=CHANNELS),
+                in0=acc[:].rearrange("p (h c) -> p h c", c=CHANNELS).unsqueeze(1).to_broadcast(shape),
+                in1=factors[:].unsqueeze(2).to_broadcast(shape),
             )
-            by_parity = acc[:].rearrange("p (h i e) -> p e h i", i=PAIRS, e=2)
-            crossed = work.tile([P, 2, width // 2], F32, tag="crossed")
-            for e in range(2):
-                nc.vector.tensor_mul(
-                    out=crossed[:, e, :].rearrange("p (h i) -> p h i", i=PAIRS),
-                    in0=by_parity[:, 1 - e],
-                    in1=signed_sin[:, e, :].unsqueeze(1).to_broadcast([P, heads, PAIRS]),
-                )
-            return straight, crossed
+            return (both,)
 
-        def add(piece, straight, crossed):
+        def add(piece, both):
             bank, start, width = piece
             w, first = banks[bank]
             nc.vector.tensor_add(
                 out=results[w][:, first + start : first + start + width].rearrange(
                     "p (m e) -> p m e", e=2
                 ),
-                in0=straight[:].rearrange("p (m e) -> p m e", e=2),
-                in1=crossed[:].rearrange("p e m -> p m e"),
+                in0=both[:, 0, :].rearrange("p (m e) -> p m e", e=2),
+                in1=both[:, 1, :].rearrange("p (m e) -> p m e", e=2)[:, :, ::-1],
             )
 
         def store(w, begin, end):
             out_rows = outputs[w].rearrange("b h t c -> b (h t c)")
             nc.sync.dma_start(out=out_rows[:, begin:end], in_=results[w][:, begin:end])
 
-        last = len(banks) - 1
         pieces = []
         products = []
 
@@ -221,24 +217,25 @@ def tile_multiscaleretention_pa_kernel(
             add(piece, *products[len(products) - 2])
             bank, start, width = piece
             w, first = banks[bank]
-            if start + width == DIRECT and bank < last:
+            if start + width == direct_of(bank) and bank < last:
                 if w == 1:
                     store(w, first, first + BANK)
                 elif first + BANK == WIDTH:
                     store(w, 0, WIDTH)
 
         for bank in range(len(banks)):
-            blocks = [turned_passes(bank, j) for j in range(TURNED // P)]
-            widths = [DIRECT] if bank < last else [P] * (DIRECT // P)
+            turned_blocks = (BANK - direct_of(bank)) // P
+            blocks = [turned_passes(bank, j) for j in range(turned_blocks)]
+            widths = [2 * P, P] if bank < last else [P] * (direct_of(bank) // P)
             for i, width in enumerate(widths):
                 piece = (bank, sum(widths[:i]), width)
                 pieces.append(piece)
                 products.append(multiply(piece, direct_passes(piece)))
                 if len(products) > 1:
                     add_previous()
-            for j in range(TURNED // P):
+            for j in range(turned_blocks):
                 rotate(bank, j, blocks[j])
         w, first = banks[last]
-        store(w, first + DIRECT, first + BANK)
+        store(w, first + direct_of(last), first + BANK)
         add(pieces[-1], *products[-1])
-        store(w, first, first + DIRECT)
+        store(w, first, first + direct_of(last))

@@ -78,7 +78,7 @@ def tile_multiscaleretention_pa_kernel(
                 ].bitcast(I32),
             )
             words.append(bank_words)
-            if first == 0:
+            if first == (BANK if w == 0 else 0):
                 for quadrant in range(QUADRANTS):
                     top = 32 * quadrant
                     nc.sync.dma_start(

@@ -38,7 +38,7 @@ def tile_multiscaleretention_pa_kernel(
 
     with ExitStack() as ctx:
         keep = ctx.enter_context(tc.tile_pool(name="keep", bufs=1))
-        words_pool = ctx.enter_context(tc.tile_pool(name="words", bufs=len(banks)))
+        words_pool = ctx.enter_context(tc.tile_pool(name="words", bufs=4))
         work = ctx.enter_context(tc.tile_pool(name="work", bufs=4))
         psum_direct = ctx.enter_context(tc.psum_pool(name="psum_direct", bufs=3))
         psum_turned = ctx.enter_context(tc.psum_pool(name="psum_turned", bufs=2))
@@ -67,18 +67,20 @@ def tile_multiscaleretention_pa_kernel(
         x_sb = keep.tile([P, E], BF16)
         nc.sync.dma_start(out=x_sb[:], in_=x.rearrange("b t e -> b (t e)"))
 
+        loads = [(0, 0, 2 * BANK), (0, 2 * BANK, BANK)] + [(1, first, BANK) for first in range(0, WIDTH, BANK)]
         words = []
-        for w, first in banks:
+        for w, first, columns in loads:
             w_words, w_scales = weights[w]
-            bank_words = words_pool.tile([P, PASSES, BANK], U32, align_bytes=64)
+            load_words = words_pool.tile([P, PASSES, columns], U32, align_bytes=64, tag="words_%d" % columns)
             nc.sync.dma_start(
-                out=bank_words[:].bitcast(I32),
+                out=load_words[:].bitcast(I32),
                 in_=w_words.rearrange("g p n t -> p g (n t)")[
-                    :, :, PACK * first : PACK * (first + BANK)
+                    :, :, PACK * first : PACK * (first + columns)
                 ].bitcast(I32),
             )
-            words.append(bank_words)
-            if first == (BANK if w == 0 else 0):
+            for offset in range(0, columns, BANK):
+                words.append((load_words, offset))
+            if first == 0:
                 for quadrant in range(QUADRANTS):
                     top = 32 * quadrant
                     nc.sync.dma_start(
@@ -149,7 +151,9 @@ def tile_multiscaleretention_pa_kernel(
             for g in range(PASSES):
                 nc.tensor.matmul_mx(
                     out=turned[:],
-                    lhsT=words[bank][:, g, column : column + P].bitcast(FP8X4),
+                    lhsT=words[bank][0][
+                        :, g, words[bank][1] + column : words[bank][1] + column + P
+                    ].bitcast(FP8X4),
                     lhsT_scale=planes[SCALE_ROWS * g : P, w, first + column : first + column + P],
                     rhs=x_codes[:, g, :].bitcast(FP8X4),
                     rhs_scale=x_scales[:, g, :],
@@ -176,7 +180,9 @@ def tile_multiscaleretention_pa_kernel(
                     out=acc[:],
                     lhsT=x_codes[:, g, :].bitcast(FP8X4),
                     lhsT_scale=x_scales[:, g, :],
-                    rhs=words[bank][:, g, start : start + width].bitcast(FP8X4),
+                    rhs=words[bank][0][
+                        :, g, words[bank][1] + start : words[bank][1] + start + width
+                    ].bitcast(FP8X4),
                     rhs_scale=planes[SCALE_ROWS * g : P, w, first + start : first + start + width],
                     start=(g == 0),
                     stop=(g == PASSES - 1),
@@ -209,33 +215,28 @@ def tile_multiscaleretention_pa_kernel(
             out_rows = outputs[w].rearrange("b h t c -> b (h t c)")
             nc.sync.dma_start(out=out_rows[:, begin:end], in_=results[w][:, begin:end])
 
-        pieces = []
-        products = []
-
-        def add_previous():
-            piece = pieces[len(products) - 2]
-            add(piece, *products[len(products) - 2])
-            bank, start, width = piece
+        pieces_of = [
+            [(bank, P * 2 * i, width) for i, width in enumerate([2 * P, P])]
+            if bank < last
+            else [(bank, P * i, P) for i in range(direct_of(bank) // P)]
+            for bank in range(len(banks))
+        ]
+        for bank in range(len(banks)):
             w, first = banks[bank]
-            if start + width == direct_of(bank) and bank < last:
+            turned_blocks = (BANK - direct_of(bank)) // P
+            blocks = [turned_passes(bank, j) for j in range(turned_blocks)]
+            products = [multiply(piece, direct_passes(piece)) for piece in pieces_of[bank]]
+            for piece, product in zip(pieces_of[bank], products):
+                add(piece, *product)
+            if bank < last:
+                for j in range(turned_blocks):
+                    rotate(bank, j, blocks[j])
                 if w == 1:
                     store(w, first, first + BANK)
                 elif first + BANK == WIDTH:
                     store(w, 0, WIDTH)
-
-        for bank in range(len(banks)):
-            turned_blocks = (BANK - direct_of(bank)) // P
-            blocks = [turned_passes(bank, j) for j in range(turned_blocks)]
-            widths = [2 * P, P] if bank < last else [P] * (direct_of(bank) // P)
-            for i, width in enumerate(widths):
-                piece = (bank, sum(widths[:i]), width)
-                pieces.append(piece)
-                products.append(multiply(piece, direct_passes(piece)))
-                if len(products) > 1:
-                    add_previous()
-            for j in range(turned_blocks):
-                rotate(bank, j, blocks[j])
-        w, first = banks[last]
-        store(w, first + direct_of(last), first + BANK)
-        add(pieces[-1], *products[-1])
-        store(w, first, first + direct_of(last))
+            else:
+                store(w, first, first + direct_of(bank))
+                for j in range(turned_blocks):
+                    rotate(bank, j, blocks[j])
+                store(w, first + direct_of(bank), first + BANK)

@@ -221,20 +221,31 @@ def tile_multiscaleretention_pa_kernel(
             else [(bank, P * i, P) for i in range(direct_of(bank) // P)]
             for bank in range(len(banks))
         ]
+        def finish(bank, blocks):
+            w, first = banks[bank]
+            for j in range(len(blocks)):
+                rotate(bank, j, blocks[j])
+            if w == 1:
+                store(w, first, first + BANK)
+            elif first + BANK == WIDTH:
+                store(w, 0, WIDTH)
+
+        LAGGED = 3
+        waiting = []
         for bank in range(len(banks)):
             w, first = banks[bank]
             turned_blocks = (BANK - direct_of(bank)) // P
             blocks = [turned_passes(bank, j) for j in range(turned_blocks)]
+            for late in waiting:
+                finish(*late)
+            waiting = []
             products = [multiply(piece, direct_passes(piece)) for piece in pieces_of[bank]]
             for piece, product in zip(pieces_of[bank], products):
                 add(piece, *product)
-            if bank < last:
-                for j in range(turned_blocks):
-                    rotate(bank, j, blocks[j])
-                if w == 1:
-                    store(w, first, first + BANK)
-                elif first + BANK == WIDTH:
-                    store(w, 0, WIDTH)
+            if bank < LAGGED:
+                waiting = [(bank, blocks)]
+            elif bank < last:
+                finish(bank, blocks)
             else:
                 store(w, first, first + direct_of(bank))
                 for j in range(turned_blocks):

@@ -250,4 +250,8 @@ def tile_multiscaleretention_pa_kernel(
                 store(w, first, first + direct_of(bank))
                 for j in range(turned_blocks):
                     rotate(bank, j, blocks[j])
-                store(w, first + direct_of(bank), first + BANK)
+                out_rows = outputs[w].rearrange("b h t c -> b (h t c)")
+                nc.scalar.dma_start(
+                    out=out_rows[:, first + direct_of(bank) : first + BANK],
+                    in_=results[w][:, first + direct_of(bank) : first + BANK],
+                )

@@ -61,11 +61,10 @@ def tile_multiscaleretention_pa_kernel(
         nc.gpsimd.tensor_scalar_mul(out=swap_pairs[:, :, 0], in0=identity_pairs[:, :, 1], scalar1=-1.0)
         nc.gpsimd.tensor_copy(out=swap_pairs[:, :, 1], in_=identity_pairs[:, :, 0])
 
-        nc.scalar.dma_start(out=table_row[0:1, 0:CHANNELS], in_=sin)
-        nc.scalar.dma_start(out=table_row[0:1, CHANNELS : 2 * CHANNELS], in_=cos)
-
         x_sb = keep.tile([P, E], BF16)
         nc.sync.dma_start(out=x_sb[:], in_=x.rearrange("b t e -> b (t e)"))
+        nc.sync.dma_start(out=table_row[0:1, 0:CHANNELS], in_=sin)
+        nc.sync.dma_start(out=table_row[0:1, CHANNELS : 2 * CHANNELS], in_=cos)
 
         loads = [(0, 0, 2 * BANK), (0, 2 * BANK, BANK)] + [(1, first, BANK) for first in range(0, WIDTH, BANK)]
         words = []

@@ -22,7 +22,6 @@ BANK = 512
 SCALE_ROWS = 4
 QUADRANTS = 4
 TURNED = 128
-TURNED_LAST = 256
 
 FLOPS = 2 * P * E * 2 * WIDTH
 
@@ -34,7 +33,12 @@ def tile_multiscaleretention_pa_kernel(
     weights = ((Wq_words, Wq_scales), (Wk_words, Wk_scales))
     outputs = (out_0, out_1)
 
-    banks = [(w, first) for w in range(2) for first in range(0, WIDTH, BANK)]
+    loads = [(0, 0, (512, 512)), (0, 1024, (512,)), (1, 0, (512,)), (1, 512, (512,)), (1, 1024, (256,)), (1, 1280, (256,))]
+    units = []
+    for w, first, widths in loads:
+        for width in widths:
+            units.append((w, first, width))
+            first += width
 
     with ExitStack() as ctx:
         keep = ctx.enter_context(tc.tile_pool(name="keep", bufs=1))
@@ -66,9 +70,9 @@ def tile_multiscaleretention_pa_kernel(
         nc.sync.dma_start(out=table_row[0:1, 0:CHANNELS], in_=sin)
         nc.sync.dma_start(out=table_row[0:1, CHANNELS : 2 * CHANNELS], in_=cos)
 
-        loads = [(0, 0, 2 * BANK), (0, 2 * BANK, BANK)] + [(1, first, BANK) for first in range(0, WIDTH, BANK)]
         words = []
-        for w, first, columns in loads:
+        for w, first, widths in loads:
+            columns = sum(widths)
             w_words, w_scales = weights[w]
             load_words = words_pool.tile([P, PASSES, columns], U32, align_bytes=64, tag="words_%d" % columns)
             nc.sync.dma_start(
@@ -77,8 +81,8 @@ def tile_multiscaleretention_pa_kernel(
                     :, :, PACK * first : PACK * (first + columns)
                 ].bitcast(I32),
             )
-            for offset in range(0, columns, BANK):
-                words.append((load_words, offset))
+            for i in range(len(widths)):
+                words.append((load_words, sum(widths[:i])))
             if first == 0:
                 for quadrant in range(QUADRANTS):
                     top = 32 * quadrant
@@ -138,13 +142,13 @@ def tile_multiscaleretention_pa_kernel(
         rotation = keep.tile([P, P], F32)
         nc.vector.tensor_add(out=rotation[:], in0=on_diagonal[:], in1=beside[:])
 
-        last = len(banks) - 1
+        last = len(units) - 1
 
         def direct_of(bank):
-            return BANK - (TURNED_LAST if bank == last else TURNED)
+            return units[bank][2] - TURNED
 
         def turned_passes(bank, j):
-            w, first = banks[bank]
+            w, first, columns = units[bank]
             column = direct_of(bank) + P * j
             turned = psum_turned.tile([P, P], F32, tag="turned")
             for g in range(PASSES):
@@ -164,7 +168,7 @@ def tile_multiscaleretention_pa_kernel(
             return turned_sb
 
         def rotate(bank, j, turned_sb):
-            w, first = banks[bank]
+            w, first, columns = units[bank]
             column = first + direct_of(bank) + P * j
             rotated = psum_rotated.tile([P, P], F32, tag="rotated")
             nc.tensor.matmul(out=rotated[:], lhsT=turned_sb[:], rhs=rotation[:], start=True, stop=True)
@@ -172,7 +176,7 @@ def tile_multiscaleretention_pa_kernel(
 
         def direct_passes(piece):
             bank, start, width = piece
-            w, first = banks[bank]
+            w, first, columns = units[bank]
             acc = psum_direct.tile([P, width], F32, tag="direct")
             for g in range(PASSES):
                 nc.tensor.matmul_mx(
@@ -201,7 +205,7 @@ def tile_multiscaleretention_pa_kernel(
 
         def add(piece, both):
             bank, start, width = piece
-            w, first = banks[bank]
+            w, first, columns = units[bank]
             nc.vector.tensor_add(
                 out=results[w][:, first + start : first + start + width].rearrange(
                     "p (m e) -> p m e", e=2
@@ -215,33 +219,37 @@ def tile_multiscaleretention_pa_kernel(
             nc.sync.dma_start(out=out_rows[:, begin:end], in_=results[w][:, begin:end])
 
         pieces_of = [
-            [(bank, P * 2 * i, width) for i, width in enumerate([2 * P, P])]
-            if bank < last
-            else [(bank, P * i, P) for i in range(direct_of(bank) // P)]
-            for bank in range(len(banks))
+            [
+                (bank, start, min(2 * P, direct_of(bank) - start))
+                for start in range(0, direct_of(bank), 2 * P)
+            ]
+            for bank in range(len(units))
         ]
         def finish(bank, blocks):
-            w, first = banks[bank]
+            w, first, columns = units[bank]
             for j in range(len(blocks)):
                 rotate(bank, j, blocks[j])
             if w == 1:
-                store(w, first, first + BANK)
-            elif first + BANK == WIDTH:
+                store(w, first, first + columns)
+            elif first + columns == WIDTH:
                 store(w, 0, WIDTH)
 
         LAGGED = 3
         waiting = []
-        for bank in range(len(banks)):
-            w, first = banks[bank]
-            turned_blocks = (BANK - direct_of(bank)) // P
+        for bank in range(len(units)):
+            w, first, columns = units[bank]
+            turned_blocks = TURNED // P
             blocks = [turned_passes(bank, j) for j in range(turned_blocks)]
+            if bank == last:
+                products = [multiply(piece, direct_passes(piece)) for piece in pieces_of[bank]]
             for late in waiting:
                 finish(*late)
             waiting = []
-            products = [multiply(piece, direct_passes(piece)) for piece in pieces_of[bank]]
+            if bank < last:
+                products = [multiply(piece, direct_passes(piece)) for piece in pieces_of[bank]]
             for piece, product in zip(pieces_of[bank], products):
                 add(piece, *product)
-            if bank < LAGGED:
+            if bank < LAGGED or bank == last - 1:
                 waiting = [(bank, blocks)]
             elif bank < last:
                 finish(bank, blocks)
@@ -251,6 +259,6 @@ def tile_multiscaleretention_pa_kernel(
                     rotate(bank, j, blocks[j])
                 out_rows = outputs[w].rearrange("b h t c -> b (h t c)")
                 nc.scalar.dma_start(
-                    out=out_rows[:, first + direct_of(bank) : first + BANK],
-                    in_=results[w][:, first + direct_of(bank) : first + BANK],
+                    out=out_rows[:, first + direct_of(bank) : first + columns],
+                    in_=results[w][:, first + direct_of(bank) : first + columns],
                 )

from contextlib import ExitStack

import concourse.mybir as mybir
from concourse.masks import make_identity

BF16 = mybir.dt.bfloat16
F32 = mybir.dt.float32
I32 = mybir.dt.int32
U8 = mybir.dt.uint8
U32 = mybir.dt.uint32
FP8X4 = mybir.dt.float8_e4m3fn_x4

P = 128
PACK = 4
K_PASS = P * PACK
E = 1536
PASSES = E // K_PASS
WIDTH = 1536
CHANNELS = 64
PAIRS = CHANNELS // 2
BANK = 512
SCALE_ROWS = 4
QUADRANTS = 4
TURNED = 128

FLOPS = 2 * P * E * 2 * WIDTH


def tile_multiscaleretention_pa_kernel(
    tc, x, sin, cos, Wq_words, Wq_scales, Wk_words, Wk_scales, out_0, out_1
):
    nc = tc.nc
    weights = ((Wq_words, Wq_scales), (Wk_words, Wk_scales))
    outputs = (out_0, out_1)

    loads = [(0, 0, (512, 512)), (0, 1024, (512,)), (1, 0, (512,)), (1, 512, (512,)), (1, 1024, (256,)), (1, 1280, (256,))]
    units = []
    for w, first, widths in loads:
        for width in widths:
            units.append((w, first, width))
            first += width

    with ExitStack() as ctx:
        keep = ctx.enter_context(tc.tile_pool(name="keep", bufs=1))
        words_pool = ctx.enter_context(tc.tile_pool(name="words", bufs=4))
        work = ctx.enter_context(tc.tile_pool(name="work", bufs=4))
        psum_direct = ctx.enter_context(tc.psum_pool(name="psum_direct", bufs=3))
        psum_turned = ctx.enter_context(tc.psum_pool(name="psum_turned", bufs=2))
        psum_rotated = ctx.enter_context(tc.psum_pool(name="psum_rotated", bufs=2))
        psum_tables = ctx.enter_context(tc.psum_pool(name="psum_tables", bufs=1))
        ctx.enter_context(tc.manual_schedule())

        table_row = keep.tile([P, 2 * CHANNELS], BF16)
        nc.vector.memset(table_row[:], 0.0)
        planes = keep.tile([P, 2, WIDTH], U8, align_bytes=64)
        nc.vector.memset(planes[:].bitcast(I32), 0)
        ones = keep.tile([P, P], BF16)
        nc.vector.memset(ones[:], 1.0)

        identity = keep.tile([P, P], F32)
        make_identity(nc, identity[:])
        swap = keep.tile([P, P], F32)
        identity_pairs = identity[:].rearrange("p (m e) -> p m e", e=2)
        swap_pairs = swap[:].rearrange("p (m e) -> p m e", e=2)
        nc.gpsimd.tensor_scalar_mul(out=swap_pairs[:, :, 0], in0=identity_pairs[:, :, 1], scalar1=-1.0)
        nc.gpsimd.tensor_copy(out=swap_pairs[:, :, 1], in_=identity_pairs[:, :, 0])

        x_sb = keep.tile([P, E], BF16)
        nc.sync.dma_start(out=x_sb[:], in_=x.rearrange("b t e -> b (t e)"))
        nc.sync.dma_start(out=table_row[0:1, 0:CHANNELS], in_=sin)
        nc.sync.dma_start(out=table_row[0:1, CHANNELS : 2 * CHANNELS], in_=cos)

        words = []
        for w, first, widths in loads:
            columns = sum(widths)
            w_words, w_scales = weights[w]
            load_words = words_pool.tile([P, PASSES, columns], U32, align_bytes=64, tag="words_%d" % columns)
            nc.sync.dma_start(
                out=load_words[:].bitcast(I32),
                in_=w_words.rearrange("g p n t -> p g (n t)")[
                    :, :, PACK * first : PACK * (first + columns)
                ].bitcast(I32),
            )
            for i in range(len(widths)):
                words.append((load_words, sum(widths[:i])))
            if first == 0:
                for quadrant in range(QUADRANTS):
                    top = 32 * quadrant
                    nc.sync.dma_start(
                        out=planes[top : top + PASSES * SCALE_ROWS, w, :].bitcast(I32),
                        in_=w_scales[
                            :, SCALE_ROWS * quadrant : SCALE_ROWS * (quadrant + 1), :
                        ].bitcast(I32),
                    )

        x_pairs = x_sb[:].bitcast(F32)
        grouped = keep.tile([P, PASSES, P, PACK], BF16, align_bytes=64)
        x_codes = keep.tile([P, PASSES, P], U32, align_bytes=64)
        x_scales = keep.tile([P, PASSES, P], U8, align_bytes=64)
        pairs_per_pass = K_PASS // 2

        for g in range(PASSES):
            flipped = psum_direct.tile([P, 2, P], F32, tag="direct")
            for u in range(2):
                nc.tensor.transpose(
                    flipped[:, u, :],
                    x_pairs[:, pairs_per_pass * g + u : pairs_per_pass * (g + 1) : 2],
                    identity[:],
                )
            nc.scalar.copy(
                out=grouped[:, g].bitcast(F32), in_=flipped[:].rearrange("p u b -> p b u")
            )
            nc.vector.quantize_mx(
                out=x_codes[:, g, :].bitcast(FP8X4),
                scales=x_scales[:, g, :],
                in_=grouped[:, g].rearrange("p b t -> p (b t)"),
            )

        results = [keep.tile([P, WIDTH], F32, name="result_%d" % w) for w in range(2)]

        spread = psum_tables.tile([P, 2 * CHANNELS], F32)
        nc.tensor.matmul(out=spread[:], lhsT=ones[:], rhs=table_row[:], start=True, stop=True)
        factors = keep.tile([P, 2, CHANNELS], F32)
        nc.vector.tensor_copy(out=factors[:, 0, :], in_=spread[:, CHANNELS : 2 * CHANNELS])
        sin_pairs = spread[:, 0:CHANNELS].rearrange("p (i e) -> p i e", e=2)
        cross_pairs = factors[:, 1, :].rearrange("p (i e) -> p i e", e=2)
        nc.vector.tensor_copy(out=cross_pairs[:, :, 0], in_=sin_pairs[:, :, 1])
        nc.vector.tensor_scalar_mul(out=cross_pairs[:, :, 1], in0=sin_pairs[:, :, 0], scalar1=-1.0)
        two_heads = [P, P // CHANNELS, CHANNELS]
        on_diagonal = keep.tile([P, P], F32)
        nc.vector.tensor_mul(
            out=on_diagonal[:].rearrange("p (h c) -> p h c", c=CHANNELS),
            in0=identity[:].rearrange("p (h c) -> p h c", c=CHANNELS),
            in1=spread[:, CHANNELS : 2 * CHANNELS].unsqueeze(1).to_broadcast(two_heads),
        )
        beside = keep.tile([P, P], F32)
        nc.vector.tensor_mul(
            out=beside[:].rearrange("p (h c) -> p h c", c=CHANNELS),
            in0=swap[:].rearrange("p (h c) -> p h c", c=CHANNELS),
            in1=spread[:, 0:CHANNELS].unsqueeze(1).to_broadcast(two_heads),
        )
        rotation = keep.tile([P, P], F32)
        nc.vector.tensor_add(out=rotation[:], in0=on_diagonal[:], in1=beside[:])

        last = len(units) - 1

        def direct_of(bank):
            return units[bank][2] - TURNED

        def turned_passes(bank, j):
            w, first, columns = units[bank]
            column = direct_of(bank) + P * j
            turned = psum_turned.tile([P, P], F32, tag="turned")
            for g in range(PASSES):
                nc.tensor.matmul_mx(
                    out=turned[:],
                    lhsT=words[bank][0][
                        :, g, words[bank][1] + column : words[bank][1] + column + P
                    ].bitcast(FP8X4),
                    lhsT_scale=planes[SCALE_ROWS * g : P, w, first + column : first + column + P],
                    rhs=x_codes[:, g, :].bitcast(FP8X4),
                    rhs_scale=x_scales[:, g, :],
                    start=(g == 0),
                    stop=(g == PASSES - 1),
                )
            turned_sb = work.tile([P, P], F32, tag="turned_sb")
            nc.scalar.copy(out=turned_sb[:], in_=turned[:])
            return turned_sb

        def rotate(bank, j, turned_sb):
            w, first, columns = units[bank]
            column = first + direct_of(bank) + P * j
            rotated = psum_rotated.tile([P, P], F32, tag="rotated")
            nc.tensor.matmul(out=rotated[:], lhsT=turned_sb[:], rhs=rotation[:], start=True, stop=True)
            nc.scalar.copy(out=results[w][:, column : column + P], in_=rotated[:])

        def direct_passes(piece):
            bank, start, width = piece
            w, first, columns = units[bank]
            acc = psum_direct.tile([P, width], F32, tag="direct")
            for g in range(PASSES):
                nc.tensor.matmul_mx(
                    out=acc[:],
                    lhsT=x_codes[:, g, :].bitcast(FP8X4),
                    lhsT_scale=x_scales[:, g, :],
                    rhs=words[bank][0][
                        :, g, words[bank][1] + start : words[bank][1] + start + width
                    ].bitcast(FP8X4),
                    rhs_scale=planes[SCALE_ROWS * g : P, w, first + start : first + start + width],
                    start=(g == 0),
                    stop=(g == PASSES - 1),
                )
            return acc

        def multiply(piece, acc):
            width = piece[2]
            shape = [P, 2, width // CHANNELS, CHANNELS]
            both = work.tile([P, 2, width], F32, tag="both")
            nc.vector.tensor_mul(
                out=both[:].rearrange("p r (h c) -> p r h c", c=CHANNELS),
                in0=acc[:].rearrange("p (h c) -> p h c", c=CHANNELS).unsqueeze(1).to_broadcast(shape),
                in1=factors[:].unsqueeze(2).to_broadcast(shape),
            )
            return (both,)

        def add(piece, both):
            bank, start, width = piece
            w, first, columns = units[bank]
            nc.vector.tensor_add(
                out=results[w][:, first + start : first + start + width].rearrange(
                    "p (m e) -> p m e", e=2
                ),
                in0=both[:, 0, :].rearrange("p (m e) -> p m e", e=2),
                in1=both[:, 1, :].rearrange("p (m e) -> p m e", e=2)[:, :, ::-1],
            )

        def store(w, begin, end):
            out_rows = outputs[w].rearrange("b h t c -> b (h t c)")
            nc.sync.dma_start(out=out_rows[:, begin:end], in_=results[w][:, begin:end])

        pieces_of = [
            [
                (bank, start, min(2 * P, direct_of(bank) - start))
                for start in range(0, direct_of(bank), 2 * P)
            ]
            for bank in range(len(units))
        ]
        def finish(bank, blocks):
            w, first, columns = units[bank]
            for j in range(len(blocks)):
                rotate(bank, j, blocks[j])
            if w == 1:
                store(w, first, first + columns)
            elif first + columns == WIDTH:
                store(w, 0, WIDTH)

        LAGGED = 3
        waiting = []
        for bank in range(len(units)):
            w, first, columns = units[bank]
            turned_blocks = TURNED // P
            blocks = [turned_passes(bank, j) for j in range(turned_blocks)]
            if bank == last:
                products = [multiply(piece, direct_passes(piece)) for piece in pieces_of[bank]]
            for late in waiting:
                finish(*late)
            waiting = []
            if bank < last:
                products = [multiply(piece, direct_passes(piece)) for piece in pieces_of[bank]]
            for piece, product in zip(pieces_of[bank], products):
                add(piece, *product)
            if bank < LAGGED or bank == last - 1:
                waiting = [(bank, blocks)]
            elif bank < last:
                finish(bank, blocks)
            else:
                store(w, first, first + direct_of(bank))
                for j in range(turned_blocks):
                    rotate(bank, j, blocks[j])
                out_rows = outputs[w].rearrange("b h t c -> b (h t c)")
                nc.scalar.dma_start(
                    out=out_rows[:, first + direct_of(bank) : first + columns],
                    in_=results[w][:, first + direct_of(bank) : first + columns],
                )
